import numpy as np
import ml_dtypes

BF16 = ml_dtypes.bfloat16


def bf(x):
    return np.asarray(x, np.float32).astype(BF16)


def f32(x):
    return np.asarray(x, np.float32)


def f64(x):
    return np.asarray(x).astype(np.float64)


def striped(idx):
    return np.tile(idx.reshape(-1, 16).T, (8, 1))


C, S, N = 256, 512, 128


def setup_inputs():
    return {"item_emb": f32(np.random.standard_normal((C, S))), "pos_emb": f32(np.random.standard_normal((C, N))), "ln_w": f32(1.0 + 0.1 * np.random.standard_normal((C, 1))), "ln_b": f32(0.1 * np.random.standard_normal((C, 1))), "offs": striped(np.random.permutation(np.tile(np.arange(S), 2))[:N])}


def reference(item_emb, pos_emb, ln_w, ln_b, offs):
    idx = offs[:16].T.reshape(-1)
    e = f64(item_emb)[:, idx] + f64(pos_emb)
    mu = e.mean(axis=0, keepdims=True)
    d = e - mu
    var = (d * d).mean(axis=0, keepdims=True)
    return f64(ln_w) * d / np.sqrt(var) + f64(ln_b)

@@ -1,0 +1,60 @@
+import concourse.mybir as mybir
+from concourse.masks import make_identity
+
+F32 = mybir.dt.float32
+U16 = mybir.dt.uint16
+ALU = mybir.AluOpType
+ACT = mybir.ActivationFunctionType
+
+P = 128
+C, S, N = 256, 512, 128
+BLOCKS = C // P
+STATS = 6
+
+
+def tile_demorecmodel_kernel(tc, item_emb, pos_emb, ln_w, ln_b, offs, out):
+    nc = tc.nc
+    with (
+        tc.tile_pool(name="held", bufs=1) as held,
+        tc.psum_pool(name="psum", bufs=1) as psum,
+    ):
+        offsets = held.tile([P, N // 16], U16, name="offsets")
+        nc.sync.dma_start(offsets[:], offs)
+        item = [held.tile([P, S], F32, name=f"item{b}") for b in range(BLOCKS)]
+        pos = [held.tile([P, N], F32, name=f"pos{b}") for b in range(BLOCKS)]
+        for b in range(BLOCKS):
+            rows = slice(b * P, (b + 1) * P)
+            nc.sync.dma_start(pos[b][:], pos_emb[rows, :])
+            nc.sync.dma_start(item[b][:], item_emb[rows, :])
+        gain = held.tile([P, BLOCKS], F32, name="gain")
+        bias = held.tile([P, BLOCKS], F32, name="bias")
+        with nc.allow_non_contiguous_dma(reason="256 floats, one to a partition"):
+            nc.scalar.dma_start(gain[:], ln_w.rearrange("(b p) o -> p (b o)", p=P))
+            nc.scalar.dma_start(bias[:], ln_b.rearrange("(b p) o -> p (b o)", p=P))
+
+        identity = held.tile([P, P], F32, name="identity")
+        make_identity(nc, identity[:])
+
+        stats = held.tile([P, BLOCKS * STATS], F32, name="stats")
+        e_t = [psum.tile([P, P], F32, name=f"e_t{b}") for b in range(BLOCKS)]
+        for b in range(BLOCKS):
+            e = held.tile([P, N], F32, name=f"e{b}")
+            nc.vector.tensor_tensor(e[:], item[b][:].indirect(offsets[:]), pos[b][:], ALU.add)
+            nc.tensor.transpose(e_t[b][:], e[:], identity[:])
+            nc.vector.bn_stats(stats[:, b * STATS : (b + 1) * STATS], e_t[b][:])
+
+        mean_var = held.tile([P, 2], F32, name="mean_var")
+        nc.vector.bn_aggr(mean_var[:], stats[:])
+        std = held.tile([P, 1], F32, name="std")
+        nc.scalar.activation(std[:], mean_var[:, 1:2], ACT.Sqrt)
+        rstd = held.tile([P, 1], F32, name="rstd")
+        nc.vector.reciprocal(rstd[:], std[:])
+
+        for b in range(BLOCKS):
+            x_t = held.tile([P, P], F32, name=f"x_t{b}")
+            nc.vector.tensor_scalar(x_t[:], e_t[b][:], mean_var[:, 0:1], rstd[:], ALU.subtract, ALU.mult)
+            x = psum.tile([P, N], F32, name=f"x{b}")
+            nc.tensor.transpose(x[:], x_t[:], identity[:])
+            y = held.tile([P, N], F32, name=f"y{b}")
+            nc.vector.tensor_scalar(y[:], x[:], gain[:, b : b + 1], bias[:, b : b + 1], ALU.mult, ALU.add)
+            nc.sync.dma_start(out[b * P : (b + 1) * P, :], y[:])

@@ -24,13 +24,13 @@ def tile_demorecmodel_kernel(tc, item_emb, pos_emb, ln_w, ln_b, offs, out):
         pos = [held.tile([P, N], F32, name=f"pos{b}") for b in range(BLOCKS)]
         for b in range(BLOCKS):
             rows = slice(b * P, (b + 1) * P)
-            nc.sync.dma_start(pos[b][:], pos_emb[rows, :])
             nc.sync.dma_start(item[b][:], item_emb[rows, :])
+            nc.scalar.dma_start(pos[b][:], pos_emb[rows, :])
         gain = held.tile([P, BLOCKS], F32, name="gain")
         bias = held.tile([P, BLOCKS], F32, name="bias")
         with nc.allow_non_contiguous_dma(reason="256 floats, one to a partition"):
-            nc.scalar.dma_start(gain[:], ln_w.rearrange("(b p) o -> p (b o)", p=P))
-            nc.scalar.dma_start(bias[:], ln_b.rearrange("(b p) o -> p (b o)", p=P))
+            nc.sync.dma_start(gain[:], ln_w.rearrange("(b p) o -> p (b o)", p=P))
+            nc.sync.dma_start(bias[:], ln_b.rearrange("(b p) o -> p (b o)", p=P))
 
         identity = held.tile([P, P], F32, name="identity")
         make_identity(nc, identity[:])
@@ -57,4 +57,5 @@ def tile_demorecmodel_kernel(tc, item_emb, pos_emb, ln_w, ln_b, offs, out):
             nc.tensor.transpose(x[:], x_t[:], identity[:])
             y = held.tile([P, N], F32, name=f"y{b}")
             nc.vector.tensor_scalar(y[:], x[:], gain[:, b : b + 1], bias[:, b : b + 1], ALU.mult, ALU.add)
-            nc.sync.dma_start(out[b * P : (b + 1) * P, :], y[:])
+            store_queue = nc.sync if b % 2 == 0 else nc.scalar
+            store_queue.dma_start(out[b * P : (b + 1) * P, :], y[:])

@@ -10,6 +10,8 @@ P = 128
 C, S, N = 256, 512, 128
 BLOCKS = C // P
 STATS = 6
+WARM_UP = 5
+KEEP_UP = 4
 
 
 def tile_demorecmodel_kernel(tc, item_emb, pos_emb, ln_w, ln_b, offs, out):
@@ -35,6 +37,12 @@ def tile_demorecmodel_kernel(tc, item_emb, pos_emb, ln_w, ln_b, offs, out):
         identity = held.tile([P, P], F32, name="identity")
         make_identity(nc, identity[:])
 
+        ones = held.tile([P, P], F32, name="ones")
+        nc.vector.memset(ones[:], 1.0)
+        unused = psum.tile([P, P], F32, name="unused")
+        for repeat in range(WARM_UP):
+            nc.tensor.matmul(unused[:], ones[:], ones[:], start=True, stop=True)
+
         stats = held.tile([P, BLOCKS * STATS], F32, name="stats")
         e_t = [psum.tile([P, P], F32, name=f"e_t{b}") for b in range(BLOCKS)]
         for b in range(BLOCKS):
@@ -42,6 +50,8 @@ def tile_demorecmodel_kernel(tc, item_emb, pos_emb, ln_w, ln_b, offs, out):
             nc.vector.tensor_tensor(e[:], item[b][:].indirect(offsets[:]), pos[b][:], ALU.add)
             nc.tensor.transpose(e_t[b][:], e[:], identity[:])
             nc.vector.bn_stats(stats[:, b * STATS : (b + 1) * STATS], e_t[b][:])
+        for repeat in range(KEEP_UP):
+            nc.tensor.matmul(unused[:], e[:], e[:], start=True, stop=True)
 
         mean_var = held.tile([P, 2], F32, name="mean_var")
         nc.vector.bn_aggr(mean_var[:], stats[:])

@@ -10,8 +10,6 @@ P = 128
 C, S, N = 256, 512, 128
 BLOCKS = C // P
 STATS = 6
-WARM_UP = 5
-KEEP_UP = 4
 
 
 def tile_demorecmodel_kernel(tc, item_emb, pos_emb, ln_w, ln_b, offs, out):
@@ -37,12 +35,6 @@ def tile_demorecmodel_kernel(tc, item_emb, pos_emb, ln_w, ln_b, offs, out):
         identity = held.tile([P, P], F32, name="identity")
         make_identity(nc, identity[:])
 
-        ones = held.tile([P, P], F32, name="ones")
-        nc.vector.memset(ones[:], 1.0)
-        unused = psum.tile([P, P], F32, name="unused")
-        for repeat in range(WARM_UP):
-            nc.tensor.matmul(unused[:], ones[:], ones[:], start=True, stop=True)
-
         stats = held.tile([P, BLOCKS * STATS], F32, name="stats")
         e_t = [psum.tile([P, P], F32, name=f"e_t{b}") for b in range(BLOCKS)]
         for b in range(BLOCKS):
@@ -50,15 +42,11 @@ def tile_demorecmodel_kernel(tc, item_emb, pos_emb, ln_w, ln_b, offs, out):
             nc.vector.tensor_tensor(e[:], item[b][:].indirect(offsets[:]), pos[b][:], ALU.add)
             nc.tensor.transpose(e_t[b][:], e[:], identity[:])
             nc.vector.bn_stats(stats[:, b * STATS : (b + 1) * STATS], e_t[b][:])
-        for repeat in range(KEEP_UP):
-            nc.tensor.matmul(unused[:], e[:], e[:], start=True, stop=True)
 
         mean_var = held.tile([P, 2], F32, name="mean_var")
         nc.vector.bn_aggr(mean_var[:], stats[:])
-        std = held.tile([P, 1], F32, name="std")
-        nc.scalar.activation(std[:], mean_var[:, 1:2], ACT.Sqrt)
         rstd = held.tile([P, 1], F32, name="rstd")
-        nc.vector.reciprocal(rstd[:], std[:])
+        nc.scalar.activation(rstd[:], mean_var[:, 1:2], ACT.Abs_reciprocal_sqrt)
 
         for b in range(BLOCKS):
             x_t = held.tile([P, P], F32, name=f"x_t{b}")

@@ -10,6 +10,7 @@ P = 128
 C, S, N = 256, 512, 128
 BLOCKS = C // P
 STATS = 6
+WARM_UP = 5
 
 
 def tile_demorecmodel_kernel(tc, item_emb, pos_emb, ln_w, ln_b, offs, out):
@@ -34,6 +35,12 @@ def tile_demorecmodel_kernel(tc, item_emb, pos_emb, ln_w, ln_b, offs, out):
 
         identity = held.tile([P, P], F32, name="identity")
         make_identity(nc, identity[:])
+
+        ones = held.tile([P, P], F32, name="ones")
+        nc.vector.memset(ones[:], 1.0)
+        unused = psum.tile([P, P], F32, name="unused")
+        for repeat in range(WARM_UP):
+            nc.tensor.matmul(unused[:], ones[:], ones[:], start=True, stop=True)
 
         stats = held.tile([P, BLOCKS * STATS], F32, name="stats")
         e_t = [psum.tile([P, P], F32, name=f"e_t{b}") for b in range(BLOCKS)]

@@ -11,6 +11,7 @@ C, S, N = 256, 512, 128
 BLOCKS = C // P
 STATS = 6
 WARM_UP = 5
+KEEP_UP = 3
 
 
 def tile_demorecmodel_kernel(tc, item_emb, pos_emb, ln_w, ln_b, offs, out):
@@ -49,6 +50,9 @@ def tile_demorecmodel_kernel(tc, item_emb, pos_emb, ln_w, ln_b, offs, out):
             nc.vector.tensor_tensor(e[:], item[b][:].indirect(offsets[:]), pos[b][:], ALU.add)
             nc.tensor.transpose(e_t[b][:], e[:], identity[:])
             nc.vector.bn_stats(stats[:, b * STATS : (b + 1) * STATS], e_t[b][:])
+
+        for repeat in range(KEEP_UP):
+            nc.tensor.matmul(unused[:STATS, :], stats[:, 0:STATS], e[:], start=True, stop=True)
 
         mean_var = held.tile([P, 2], F32, name="mean_var")
         nc.vector.bn_aggr(mean_var[:], stats[:])

@@ -20,19 +20,19 @@ def tile_demorecmodel_kernel(tc, item_emb, pos_emb, ln_w, ln_b, offs, out):
         tc.tile_pool(name="held", bufs=1) as held,
         tc.psum_pool(name="psum", bufs=1) as psum,
     ):
+        item_blocks = item_emb.rearrange("(p b) s -> b p s", b=BLOCKS)
+
         offsets = held.tile([P, N // 16], U16, name="offsets")
         nc.sync.dma_start(offsets[:], offs)
         item = [held.tile([P, S], F32, name=f"item{b}") for b in range(BLOCKS)]
-        pos = [held.tile([P, N], F32, name=f"pos{b}") for b in range(BLOCKS)]
+        pos = held.tile([P, BLOCKS, N], F32, name="pos")
+        nc.scalar.dma_start(pos[:], pos_emb.rearrange("(p b) n -> p b n", b=BLOCKS))
         for b in range(BLOCKS):
-            rows = slice(b * P, (b + 1) * P)
-            nc.sync.dma_start(item[b][:], item_emb[rows, :])
-            nc.scalar.dma_start(pos[b][:], pos_emb[rows, :])
+            nc.sync.dma_start(item[b][:], item_blocks[b])
         gain = held.tile([P, BLOCKS], F32, name="gain")
         bias = held.tile([P, BLOCKS], F32, name="bias")
-        with nc.allow_non_contiguous_dma(reason="256 floats, one to a partition"):
-            nc.sync.dma_start(gain[:], ln_w.rearrange("(b p) o -> p (b o)", p=P))
-            nc.sync.dma_start(bias[:], ln_b.rearrange("(b p) o -> p (b o)", p=P))
+        nc.sync.dma_start(gain[:], ln_w.rearrange("(p b) o -> p (b o)", b=BLOCKS))
+        nc.sync.dma_start(bias[:], ln_b.rearrange("(p b) o -> p (b o)", b=BLOCKS))
 
         identity = held.tile([P, P], F32, name="identity")
         make_identity(nc, identity[:])
@@ -47,7 +47,7 @@ def tile_demorecmodel_kernel(tc, item_emb, pos_emb, ln_w, ln_b, offs, out):
         e_t = [psum.tile([P, P], F32, name=f"e_t{b}") for b in range(BLOCKS)]
         for b in range(BLOCKS):
             e = held.tile([P, N], F32, name=f"e{b}")
-            nc.vector.tensor_tensor(e[:], item[b][:].indirect(offsets[:]), pos[b][:], ALU.add)
+            nc.vector.tensor_tensor(e[:], item[b][:].indirect(offsets[:]), pos[:, b, :], ALU.add)
             nc.tensor.transpose(e_t[b][:], e[:], identity[:])
             nc.vector.bn_stats(stats[:, b * STATS : (b + 1) * STATS], e_t[b][:])
 
@@ -59,12 +59,11 @@ def tile_demorecmodel_kernel(tc, item_emb, pos_emb, ln_w, ln_b, offs, out):
         rstd = held.tile([P, 1], F32, name="rstd")
         nc.scalar.activation(rstd[:], mean_var[:, 1:2], ACT.Abs_reciprocal_sqrt)
 
+        y = held.tile([P, BLOCKS, N], F32, name="y")
         for b in range(BLOCKS):
             x_t = held.tile([P, P], F32, name=f"x_t{b}")
             nc.vector.tensor_scalar(x_t[:], e_t[b][:], mean_var[:, 0:1], rstd[:], ALU.subtract, ALU.mult)
             x = psum.tile([P, N], F32, name=f"x{b}")
             nc.tensor.transpose(x[:], x_t[:], identity[:])
-            y = held.tile([P, N], F32, name=f"y{b}")
-            nc.vector.tensor_scalar(y[:], x[:], gain[:, b : b + 1], bias[:, b : b + 1], ALU.mult, ALU.add)
-            store_queue = nc.sync if b % 2 == 0 else nc.scalar
-            store_queue.dma_start(out[b * P : (b + 1) * P, :], y[:])
+            nc.vector.tensor_scalar(y[:, b, :], x[:], gain[:, b : b + 1], bias[:, b : b + 1], ALU.mult, ALU.add)
+        nc.sync.dma_start(out.rearrange("(p b) n -> p b n", b=BLOCKS), y[:])

@@ -31,8 +31,8 @@ def tile_demorecmodel_kernel(tc, item_emb, pos_emb, ln_w, ln_b, offs, out):
             nc.sync.dma_start(item[b][:], item_blocks[b])
         gain = held.tile([P, BLOCKS], F32, name="gain")
         bias = held.tile([P, BLOCKS], F32, name="bias")
-        nc.sync.dma_start(gain[:], ln_w.rearrange("(p b) o -> p (b o)", b=BLOCKS))
-        nc.sync.dma_start(bias[:], ln_b.rearrange("(p b) o -> p (b o)", b=BLOCKS))
+        nc.scalar.dma_start(gain[:], ln_w.rearrange("(p b) o -> p (b o)", b=BLOCKS))
+        nc.scalar.dma_start(bias[:], ln_b.rearrange("(p b) o -> p (b o)", b=BLOCKS))
 
         identity = held.tile([P, P], F32, name="identity")
         make_identity(nc, identity[:])

@@ -21,6 +21,7 @@ def tile_demorecmodel_kernel(tc, item_emb, pos_emb, ln_w, ln_b, offs, out):
         tc.psum_pool(name="psum", bufs=1) as psum,
     ):
         item_blocks = item_emb.rearrange("(p b) s -> b p s", b=BLOCKS)
+        out_blocks = out.rearrange("(p b) n -> b p n", b=BLOCKS)
 
         offsets = held.tile([P, N // 16], U16, name="offsets")
         nc.sync.dma_start(offsets[:], offs)
@@ -66,4 +67,5 @@ def tile_demorecmodel_kernel(tc, item_emb, pos_emb, ln_w, ln_b, offs, out):
             x = psum.tile([P, N], F32, name=f"x{b}")
             nc.tensor.transpose(x[:], x_t[:], identity[:])
             nc.vector.tensor_scalar(y[:, b, :], x[:], gain[:, b : b + 1], bias[:, b : b + 1], ALU.mult, ALU.add)
-        nc.sync.dma_start(out.rearrange("(p b) n -> p b n", b=BLOCKS), y[:])
+            store_queue = nc.scalar if b == 0 else nc.sync
+            store_queue.dma_start(out_blocks[b], y[:, b, :])

import concourse.mybir as mybir
from concourse.masks import make_identity

F32 = mybir.dt.float32
U16 = mybir.dt.uint16
ALU = mybir.AluOpType
ACT = mybir.ActivationFunctionType

P = 128
C, S, N = 256, 512, 128
BLOCKS = C // P
STATS = 6
WARM_UP = 5
KEEP_UP = 3


def tile_demorecmodel_kernel(tc, item_emb, pos_emb, ln_w, ln_b, offs, out):
    nc = tc.nc
    with (
        tc.tile_pool(name="held", bufs=1) as held,
        tc.psum_pool(name="psum", bufs=1) as psum,
    ):
        item_blocks = item_emb.rearrange("(p b) s -> b p s", b=BLOCKS)
        out_blocks = out.rearrange("(p b) n -> b p n", b=BLOCKS)

        offsets = held.tile([P, N // 16], U16, name="offsets")
        nc.sync.dma_start(offsets[:], offs)
        item = [held.tile([P, S], F32, name=f"item{b}") for b in range(BLOCKS)]
        pos = held.tile([P, BLOCKS, N], F32, name="pos")
        nc.scalar.dma_start(pos[:], pos_emb.rearrange("(p b) n -> p b n", b=BLOCKS))
        for b in range(BLOCKS):
            nc.sync.dma_start(item[b][:], item_blocks[b])
        gain = held.tile([P, BLOCKS], F32, name="gain")
        bias = held.tile([P, BLOCKS], F32, name="bias")
        nc.scalar.dma_start(gain[:], ln_w.rearrange("(p b) o -> p (b o)", b=BLOCKS))
        nc.scalar.dma_start(bias[:], ln_b.rearrange("(p b) o -> p (b o)", b=BLOCKS))

        identity = held.tile([P, P], F32, name="identity")
        make_identity(nc, identity[:])

        ones = held.tile([P, P], F32, name="ones")
        nc.vector.memset(ones[:], 1.0)
        unused = psum.tile([P, P], F32, name="unused")
        for repeat in range(WARM_UP):
            nc.tensor.matmul(unused[:], ones[:], ones[:], start=True, stop=True)

        stats = held.tile([P, BLOCKS * STATS], F32, name="stats")
        e_t = [psum.tile([P, P], F32, name=f"e_t{b}") for b in range(BLOCKS)]
        for b in range(BLOCKS):
            e = held.tile([P, N], F32, name=f"e{b}")
            nc.vector.tensor_tensor(e[:], item[b][:].indirect(offsets[:]), pos[:, b, :], ALU.add)
            nc.tensor.transpose(e_t[b][:], e[:], identity[:])
            nc.vector.bn_stats(stats[:, b * STATS : (b + 1) * STATS], e_t[b][:])

        for repeat in range(KEEP_UP):
            nc.tensor.matmul(unused[:STATS, :], stats[:, 0:STATS], e[:], start=True, stop=True)

        mean_var = held.tile([P, 2], F32, name="mean_var")
        nc.vector.bn_aggr(mean_var[:], stats[:])
        rstd = held.tile([P, 1], F32, name="rstd")
        nc.scalar.activation(rstd[:], mean_var[:, 1:2], ACT.Abs_reciprocal_sqrt)

        y = held.tile([P, BLOCKS, N], F32, name="y")
        for b in range(BLOCKS):
            x_t = held.tile([P, P], F32, name=f"x_t{b}")
            nc.vector.tensor_scalar(x_t[:], e_t[b][:], mean_var[:, 0:1], rstd[:], ALU.subtract, ALU.mult)
            x = psum.tile([P, N], F32, name=f"x{b}")
            nc.tensor.transpose(x[:], x_t[:], identity[:])
            nc.vector.tensor_scalar(y[:, b, :], x[:], gain[:, b : b + 1], bias[:, b : b + 1], ALU.mult, ALU.add)
            store_queue = nc.scalar if b == 0 else nc.sync
            store_queue.dma_start(out_blocks[b], y[:, b, :])
